import numpy as np
import ml_dtypes


def mxq(x, axis, fmt="e4m3"):
    dtype, down = {"e4m3": (ml_dtypes.float8_e4m3fn, 7), "e5m2": (ml_dtypes.float8_e5m2, 14)}[fmt]
    v = np.moveaxis(np.asarray(x, np.float32).astype(ml_dtypes.bfloat16).astype(np.float64), axis, -1)
    blocks = v.reshape(v.shape[:-1] + (-1, 32))
    amax = np.abs(blocks).max(-1, keepdims=True)
    byte = np.maximum(np.where(amax > 0, np.frexp(amax)[1] - 1 + 127, 0) - down, 1)
    scale = np.exp2(byte - 127.0)
    codes = (blocks / scale).astype(np.float32).astype(dtype).astype(np.float64)
    return np.moveaxis((codes * scale).reshape(v.shape), -1, axis)


WIDE = False


def mx_kscale(k):
    if not WIDE:
        return np.ones(k)
    levels = np.array([10, -10, 5, -5, 0])
    if k % 512:
        return np.exp2(np.random.permutation(np.resize(levels, k // 32))).repeat(32)
    a = np.empty((k // 512, 16))
    for p in range(k // 512):
        a[p, :8] = np.random.permutation(np.resize(levels, 8))
        for g in range(8):
            far = levels[np.abs(levels - a[p, g]) >= 10]
            a[p, g + 8] = far[np.random.randint(len(far))]
    return np.exp2(a.ravel()).repeat(32)


BF16 = ml_dtypes.bfloat16


def bf(x):
    return np.asarray(x, np.float32).astype(BF16)


def f64(x):
    return np.asarray(x).astype(np.float64)


E2M1 = np.array([0.0, 0.5, 1.0, 1.5, 2.0, 3.0, 4.0, 6.0, -0.0, -0.5, -1.0, -1.5, -2.0, -3.0, -4.0, -6.0])


def pack_weight(w, fmt):
    k, n = w.shape
    w = f64(bf(w)).reshape(k // 32, 32, n)
    amax = np.abs(w).max(1)
    if fmt == "e4m3":
        byte = np.frexp(amax)[1] - 1 + 127 - 7
    else:
        mant, ex = np.frexp(amax / 6.0)
        byte = np.where(mant > 0.5, ex, ex - 1) + 127
    byte = np.clip(np.where(amax > 0, byte, 1), 1, 254)
    scaled = (w * np.exp2(127.0 - byte)[:, None, :]).reshape(k, n).astype(np.float32)
    by_word = np.ascontiguousarray(scaled.reshape(k // 512, 128, 4, n).transpose(0, 1, 3, 2))
    if fmt == "e4m3":
        words = by_word.astype(ml_dtypes.float8_e4m3fn).view(np.uint8)
    else:
        c = by_word.astype(ml_dtypes.float4_e2m1fn).view(np.uint8) & 0xF
        words = c[..., 0::2] | (c[..., 1::2] << 4)
    return np.ascontiguousarray(words), np.ascontiguousarray(byte.astype(np.uint8).reshape(k // 512, 16, n))


def unpack_weight(words, scales, fmt):
    g, p, n, _ = words.shape
    if fmt == "e4m3":
        vals = np.ascontiguousarray(words).view(ml_dtypes.float8_e4m3fn).astype(np.float64)
    else:
        nib = np.empty((g, p, n, 4), np.uint8)
        nib[..., 0::2] = words & 0xF
        nib[..., 1::2] = words >> 4
        vals = E2M1[nib]
    vals = vals * np.repeat(np.exp2(scales.astype(np.float64) - 127.0), 8, axis=1)[..., None]
    return vals.transpose(0, 1, 3, 2).reshape(g * 512, n)
def pack4(w):
    words, scales = pack_weight(w, "e2m1")
    return words.reshape(words.shape[0], 128, -1), scales


def unpack4(words, scales):
    return unpack_weight(words.reshape(words.shape[0], 128, -1, 2), scales, "e2m1")


B, T, C, H, KH, D = 4, 128, 2048, 16, 4, 128
HD = H * D


def sigmoid(v):
    return 1.0 / (1.0 + np.exp(-v))


def draw0():
    s, t = mx_kscale(C), mx_kscale(HD)
    x = bf(np.random.standard_normal((B, T, C)) * s)
    y_attn = bf((np.random.standard_normal((B, T, HD)) * 0.3 * t).reshape(B, T, H, D))
    w_gate_words, w_gate_scales = pack4(np.random.standard_normal((C, HD)) / np.sqrt(C) / s[:, None])
    w_proj_words, w_proj_scales = pack4(np.random.standard_normal((HD, C)) * 3.0 / np.sqrt(HD) / t[:, None])
    return {"x": x,
            "y_attn": y_attn,
            "w_gate_words": w_gate_words,
            "w_gate_scales": w_gate_scales,
            "w_proj_words": w_proj_words,
            "w_proj_scales": w_proj_scales}


def core(x, y_attn, w_gate_words, w_gate_scales, w_proj_words, w_proj_scales):
    gate = sigmoid((mxq(f64(x), 2, "e4m3") @ unpack4(w_gate_words, w_gate_scales)).reshape(B, T, H, D))
    y = f64(y_attn) * gate
    return mxq(y.reshape(B, T, HD), 2, "e4m3") @ unpack4(w_proj_words, w_proj_scales)


def e4m3fn_bytes(y):
    return np.clip(np.asarray(y, np.float64), -448.0, 448.0).astype(np.float32).astype(ml_dtypes.float8_e4m3fn).view(np.uint8)


def e4m3fn_values(b):
    return np.asarray(b, np.uint8).view(ml_dtypes.float8_e4m3fn).astype(np.float64)


def setup_inputs():
    d = draw0()
    x0 = np.asarray(d['x']).astype(np.float64)
    s = (np.max(np.abs(x0), axis=(0, 1), keepdims=True) / 448.0).astype(np.float32)
    out = {}
    for k, v in d.items():
        if k == 'x':
            out['x_bytes'] = e4m3fn_bytes(x0 / s.astype(np.float64))
            out['x_scale'] = s
        else:
            out[k] = v
    return out


def reference(x_bytes, x_scale, y_attn, w_gate_words, w_gate_scales, w_proj_words, w_proj_scales):
    return core(e4m3fn_values(x_bytes) * x_scale.astype(np.float64), y_attn, w_gate_words, w_gate_scales, w_proj_words, w_proj_scales)

@@ -1,0 +1,246 @@
+from contextlib import ExitStack
+
+import concourse.mybir as mybir
+from concourse.masks import make_identity
+
+BATCH, TOKENS, K = 4, 128, 2048
+P = 128
+PACK = 4
+K_PASS = P * PACK
+PASSES = K // K_PASS
+N_TILE = 512
+CHUNKS = K // N_TILE
+
+FLOPS = 2 * 2 * BATCH * TOKENS * K * K
+
+F32 = mybir.dt.float32
+BF16 = mybir.dt.bfloat16
+I32 = mybir.dt.int32
+U32 = mybir.dt.uint32
+U8 = mybir.dt.uint8
+FP8 = mybir.dt.float8_e4m3fn
+FP8X4 = mybir.dt.float8_e4m3fn_x4
+FP4X4 = mybir.dt.float4_e2m1fn_x4
+ACT = mybir.ActivationFunctionType
+ALU = mybir.AluOpType
+
+
+def tile_multiheadattention_pb_w4_kernel(
+    tc, x_bytes, x_scale, y_attn, w_gate_words, w_gate_scales, w_proj_words, w_proj_scales, out
+):
+    nc = tc.nc
+    with ExitStack() as ctx:
+        keep = ctx.enter_context(tc.tile_pool(name="keep", bufs=1))
+        work = ctx.enter_context(tc.tile_pool(name="work", bufs=2))
+        psum = ctx.enter_context(tc.psum_pool(name="psum", bufs=4))
+        ctx.enter_context(tc.manual_schedule())
+
+        ident = keep.tile([P, P], F32, name="ident")
+        scale_x = keep.tile([P, PASSES, PACK], F32, name="scale_x")
+        warm = keep.tile([P, 1], F32, name="warm")
+        gate_w = keep.tile([P, PASSES, 2 * K], U8, name="gate_w", align_bytes=64)
+        gate_s = keep.tile([P, PASSES, K], U8, name="gate_s", align_bytes=64)
+        proj_w = keep.tile([P, PASSES, 2 * K], U8, name="proj_w", align_bytes=64)
+        proj_s = keep.tile([P, PASSES, K], U8, name="proj_s", align_bytes=64)
+        xraw = [keep.tile([P, K], U8, name="xraw%d" % m, align_bytes=64) for m in range(BATCH)]
+        y = [keep.tile([P, K], BF16, name="y%d" % m, align_bytes=64) for m in range(BATCH)]
+        xwide = [keep.tile([P, K], BF16, name="xwide%d" % m, align_bytes=64) for m in range(BATCH)]
+        xcodes = [keep.tile([P, PASSES, TOKENS], U32, name="xcodes%d" % m, align_bytes=64) for m in range(BATCH)]
+        xplane = [keep.tile([P, PASSES, TOKENS], U8, name="xplane%d" % m, align_bytes=64) for m in range(BATCH)]
+        hcodes = [keep.tile([P, PASSES, TOKENS], U32, name="hcodes%d" % m, align_bytes=64) for m in range(BATCH)]
+        hplane = [keep.tile([P, PASSES, TOKENS], U8, name="hplane%d" % m, align_bytes=64) for m in range(BATCH)]
+
+        def load_scales(plane, scales):
+            for q in range(4):
+                nc.sync.dma_start(
+                    out=plane[32 * q : 32 * q + 4, :, :].bitcast(I32),
+                    in_=scales[:, 4 * q : 4 * q + 4, :].rearrange("g q n -> q g n").bitcast(I32),
+                )
+
+        nc.vector.memset(gate_s[:].rearrange("p g n -> p (g n)").bitcast(I32), 0)
+        nc.vector.memset(warm[:], 0.0)
+        make_identity(nc, ident[:])
+        nc.scalar.dma_start(out=scale_x[:], in_=x_scale.rearrange("a b (g p t) -> p (a b g) t", p=P, t=PACK))
+        nc.scalar.activation(warm[:], warm[:], ACT.Sigmoid)
+        for half in range(2):
+            cols = slice(half * K // 2, (half + 1) * K // 2)
+            nc.sync.dma_start(out=xraw[0][:, cols], in_=x_bytes[0][:, cols])
+        load_scales(gate_s, w_gate_scales)
+        nc.sync.dma_start(out=xraw[1][:], in_=x_bytes[1])
+        for g in range(PASSES):
+            nc.sync.dma_start(out=gate_w[:, g, :], in_=w_gate_words[g])
+        nc.sync.dma_start(out=y[0][:], in_=y_attn[0].rearrange("t h d -> t (h d)"))
+        nc.sync.dma_start(out=xraw[2][:], in_=x_bytes[2])
+        nc.vector.memset(proj_s[:].rearrange("p g n -> p (g n)").bitcast(I32), 0)
+        nc.sync.dma_start(out=y[1][:], in_=y_attn[1].rearrange("t h d -> t (h d)"))
+        nc.sync.dma_start(out=xraw[3][:], in_=x_bytes[3])
+        load_scales(proj_s, w_proj_scales)
+        for g in range(PASSES):
+            nc.sync.dma_start(out=proj_w[:, g, :], in_=w_proj_words[g])
+        for m in range(2, BATCH):
+            nc.sync.dma_start(out=y[m][:], in_=y_attn[m].rearrange("t h d -> t (h d)"))
+
+        def widen(m, g, copy):
+            cols = slice(g * K_PASS, (g + 1) * K_PASS)
+            copy(out=xwide[m][:, cols], in_=xraw[m][:, cols].bitcast(FP8))
+
+        def turn_x(m, banks):
+            words = xwide[m][:].bitcast(F32)
+            for g in range(PASSES):
+                if g % 2 == 0:
+                    banks.append(psum.tile([P, 2, 2, TOKENS], F32, name="turned", tag="turned"))
+                for u in range(2):
+                    nc.tensor.transpose(
+                        banks[-1][:, g % 2, u, :], words[:, 256 * g + u : 256 * (g + 1) : 2], ident[:]
+                    )
+
+        def scale_product(m, g, banks, grouped):
+            nc.vector.tensor_tensor(
+                out=grouped[:, g * K_PASS : (g + 1) * K_PASS].rearrange("p (r u e) -> p r u e", u=2, e=2),
+                in0=banks[g // 2][:, g % 2, :, :].bitcast(BF16).rearrange("p u (r e) -> p r u e", e=2),
+                in1=scale_x[:, g, :].rearrange("p (u e) -> p u e", u=2).unsqueeze(1).to_broadcast([P, TOKENS, 2, 2]),
+                op=ALU.mult,
+            )
+
+        def quantize(codes, plane, grouped, g0, g1):
+            nc.vector.quantize_mx(
+                out=codes[:, g0:g1, :].rearrange("p g r -> p (g r)").bitcast(FP8X4),
+                scales=plane[:, g0:g1, :].rearrange("p g r -> p (g r)"),
+                in_=grouped[:, g0 * K_PASS : g1 * K_PASS],
+            )
+
+        def new_acc():
+            return psum.tile([TOKENS, N_TILE], F32, name="acc", tag="acc")
+
+        def mx_pass(acc, codes, plane, w, s, g, c):
+            nc.tensor.matmul_mx(
+                out=acc[:],
+                lhsT=codes[:, g, :].bitcast(FP8X4),
+                lhsT_scale=plane[:, g, :],
+                rhs=w[:, g, 2 * c * N_TILE : 2 * (c + 1) * N_TILE].bitcast(FP4X4),
+                rhs_scale=s[:, g, c * N_TILE : (c + 1) * N_TILE],
+                start=(g == 0),
+                stop=(g == PASSES - 1),
+            )
+
+        def gate_matmuls(m, together):
+            accs = []
+            for c0 in range(0, CHUNKS, together):
+                new = [new_acc() for c in range(together)]
+                for g in range(PASSES):
+                    for j in range(together):
+                        mx_pass(new[j], xcodes[m], xplane[m], gate_w, gate_s, g, c0 + j)
+                accs.extend(new)
+            return accs
+
+        def sigmoids(accs):
+            gates = []
+            for acc in accs:
+                gate = work.tile([TOKENS, N_TILE], F32, name="gate", tag="gate", bufs=6)
+                nc.scalar.activation(gate[:], acc[:], ACT.Sigmoid)
+                gates.append(gate)
+            return gates
+
+        def products(m, gates):
+            h = work.tile([TOKENS, K], BF16, name="h", tag="h", bufs=3, align_bytes=64)
+            for c in range(CHUNKS):
+                cols = slice(c * N_TILE, (c + 1) * N_TILE)
+                nc.vector.tensor_tensor(
+                    out=h[:, cols].rearrange("r (u p e) -> r u p e", u=2, e=2),
+                    in0=gates[c][:].rearrange("r (p u e) -> r u p e", u=2, e=2),
+                    in1=y[m][:, cols].rearrange("r (p u e) -> r u p e", u=2, e=2),
+                    op=ALU.mult,
+                )
+            return h
+
+        def turn_h(h):
+            words = h[:].bitcast(F32)
+            banks = []
+            for g in range(PASSES):
+                if g % 2 == 0:
+                    banks.append(psum.tile([P, 2, 2, TOKENS], F32, name="turned", tag="turned"))
+                for u in range(2):
+                    nc.tensor.transpose(
+                        banks[-1][:, g % 2, u, :], words[:, 256 * g + 128 * u : 256 * g + 128 * (u + 1)], ident[:]
+                    )
+            return banks
+
+        def regroup(banks, copies):
+            grouped = work.tile([P, TOKENS * K // P], BF16, name="hgrouped", tag="hgrouped", bufs=2, align_bytes=64)
+            words = grouped[:].bitcast(F32)
+            for j in range(2):
+                copies[j](
+                    out=words[:, 512 * j : 512 * (j + 1)].rearrange("p (g r u) -> p g r u", g=2, u=2),
+                    in_=banks[j][:].rearrange("p g u r -> p g r u"),
+                )
+            return grouped
+
+        def project(m):
+            for c in range(CHUNKS):
+                acc = new_acc()
+                for g in range(PASSES):
+                    mx_pass(acc, hcodes[m], hplane[m], proj_w, proj_s, g, c)
+                result = work.tile([TOKENS, N_TILE], F32, name="result", tag="result", bufs=6)
+                copy = nc.vector.tensor_copy if c % 2 == 0 else nc.scalar.copy
+                copy(out=result[:], in_=acc[:])
+                nc.sync.dma_start(out=out[m][:, c * N_TILE : (c + 1) * N_TILE], in_=result[:])
+
+        def new_xgrouped():
+            return work.tile([P, TOKENS * K // P], BF16, name="xgrouped", tag="xgrouped", bufs=2, align_bytes=64)
+
+        def prepare_x(m, banks):
+            grouped = new_xgrouped()
+            for g in range(PASSES):
+                scale_product(m, g, banks, grouped)
+                if g > 0:
+                    quantize(xcodes[m], xplane[m], grouped, g - 1, g)
+            quantize(xcodes[m], xplane[m], grouped, PASSES - 1, PASSES)
+
+        for g in range(PASSES):
+            widen(0, g, nc.vector.tensor_copy if g < 2 else nc.scalar.copy)
+        for g in range(PASSES):
+            widen(1, g, nc.scalar.copy)
+        banks0 = []
+        turn_x(0, banks0)
+        grouped0 = new_xgrouped()
+        for g in range(PASSES):
+            scale_product(0, g, banks0, grouped0)
+            quantize(xcodes[0], xplane[0], grouped0, g, g + 1)
+        banks1 = []
+        turn_x(1, banks1)
+        prepare_x(1, banks1)
+        accs0 = gate_matmuls(0, 4)
+
+        for g in range(PASSES):
+            widen(2, g, nc.scalar.copy)
+        banks2 = []
+        turn_x(2, banks2)
+        h0 = products(0, sigmoids(accs0))
+        prepare_x(2, banks2)
+        accs1 = gate_matmuls(1, 2)
+        for g in range(PASSES):
+            widen(3, g, nc.scalar.copy)
+        h1 = products(1, sigmoids(accs1))
+        hbanks0 = turn_h(h0)
+        banks3 = []
+        turn_x(3, banks3)
+        hgrouped0 = regroup(hbanks0, (nc.scalar.copy, nc.scalar.copy))
+        quantize(hcodes[0], hplane[0], hgrouped0, 0, PASSES)
+        prepare_x(3, banks3)
+        accs2 = gate_matmuls(2, 2)
+        h2 = products(2, sigmoids(accs2))
+        project(0)
+        hbanks1 = turn_h(h1)
+        hbanks2 = turn_h(h2)
+        hgrouped1 = regroup(hbanks1, (nc.scalar.copy, nc.vector.tensor_copy))
+        hgrouped2 = regroup(hbanks2, (nc.scalar.copy, nc.vector.tensor_copy))
+        quantize(hcodes[1], hplane[1], hgrouped1, 0, PASSES)
+        quantize(hcodes[2], hplane[2], hgrouped2, 0, PASSES)
+        accs3 = gate_matmuls(3, 2)
+        h3 = products(3, sigmoids(accs3))
+        project(1)
+        hbanks3 = turn_h(h3)
+        hgrouped3 = regroup(hbanks3, (nc.scalar.copy, nc.vector.tensor_copy))
+        quantize(hcodes[3], hplane[3], hgrouped3, 0, PASSES)
+        project(2)
+        project(3)

@@ -37,6 +37,7 @@ def tile_multiheadattention_pb_w4_kernel(
 
         ident = keep.tile([P, P], F32, name="ident")
         scale_x = keep.tile([P, PASSES, PACK], F32, name="scale_x")
+        zeros = keep.tile([P, N_TILE], BF16, name="zeros", align_bytes=64)
         warm = keep.tile([P, 1], F32, name="warm")
         gate_w = keep.tile([P, PASSES, 2 * K], U8, name="gate_w", align_bytes=64)
         gate_s = keep.tile([P, PASSES, K], U8, name="gate_s", align_bytes=64)
@@ -51,53 +52,65 @@ def tile_multiheadattention_pb_w4_kernel(
         hplane = [keep.tile([P, PASSES, TOKENS], U8, name="hplane%d" % m, align_bytes=64) for m in range(BATCH)]
 
         def load_scales(plane, scales):
-            for q in range(4):
+            for r in range(4):
                 nc.sync.dma_start(
-                    out=plane[32 * q : 32 * q + 4, :, :].bitcast(I32),
-                    in_=scales[:, 4 * q : 4 * q + 4, :].rearrange("g q n -> q g n").bitcast(I32),
+                    out=plane[r:P:32, :, :].bitcast(I32),
+                    in_=scales[:, r::4, :].rearrange("g q n -> q g n").bitcast(I32),
                 )
 
+        def load_words(tile, words, g0, g1):
+            nc.sync.dma_start(out=tile[:, g0:g1, :], in_=words[g0:g1].rearrange("g p b -> p g b"))
+
+        def load_y(m):
+            nc.sync.dma_start(out=y[m][:], in_=y_attn[m].rearrange("t h d -> t (h d)"))
+
+        nc.scalar.dma_start(out=scale_x[:], in_=x_scale.rearrange("a b (g p t) -> p (a b g) t", p=P, t=PACK))
+        make_identity(nc, ident[:])
+        nc.gpsimd.memset(zeros[:], 0.0)
         nc.vector.memset(gate_s[:].rearrange("p g n -> p (g n)").bitcast(I32), 0)
         nc.vector.memset(warm[:], 0.0)
-        make_identity(nc, ident[:])
-        nc.scalar.dma_start(out=scale_x[:], in_=x_scale.rearrange("a b (g p t) -> p (a b g) t", p=P, t=PACK))
         nc.scalar.activation(warm[:], warm[:], ACT.Sigmoid)
         for half in range(2):
             cols = slice(half * K // 2, (half + 1) * K // 2)
             nc.sync.dma_start(out=xraw[0][:, cols], in_=x_bytes[0][:, cols])
-        load_scales(gate_s, w_gate_scales)
         nc.sync.dma_start(out=xraw[1][:], in_=x_bytes[1])
+        load_scales(gate_s, w_gate_scales)
         for g in range(PASSES):
-            nc.sync.dma_start(out=gate_w[:, g, :], in_=w_gate_words[g])
-        nc.sync.dma_start(out=y[0][:], in_=y_attn[0].rearrange("t h d -> t (h d)"))
+            load_words(gate_w, w_gate_words, g, g + 1)
         nc.sync.dma_start(out=xraw[2][:], in_=x_bytes[2])
-        nc.vector.memset(proj_s[:].rearrange("p g n -> p (g n)").bitcast(I32), 0)
-        nc.sync.dma_start(out=y[1][:], in_=y_attn[1].rearrange("t h d -> t (h d)"))
+        load_y(0)
         nc.sync.dma_start(out=xraw[3][:], in_=x_bytes[3])
+        load_y(1)
+        nc.vector.memset(proj_s[:].rearrange("p g n -> p (g n)").bitcast(I32), 0)
         load_scales(proj_s, w_proj_scales)
-        for g in range(PASSES):
-            nc.sync.dma_start(out=proj_w[:, g, :], in_=w_proj_words[g])
+        for g in range(0, PASSES, 2):
+            load_words(proj_w, w_proj_words, g, g + 2)
         for m in range(2, BATCH):
-            nc.sync.dma_start(out=y[m][:], in_=y_attn[m].rearrange("t h d -> t (h d)"))
+            load_y(m)
 
         def widen(m, g, copy):
             cols = slice(g * K_PASS, (g + 1) * K_PASS)
             copy(out=xwide[m][:, cols], in_=xraw[m][:, cols].bitcast(FP8))
 
-        def turn_x(m, banks):
-            words = xwide[m][:].bitcast(F32)
-            for g in range(PASSES):
-                if g % 2 == 0:
-                    banks.append(psum.tile([P, 2, 2, TOKENS], F32, name="turned", tag="turned"))
-                for u in range(2):
-                    nc.tensor.transpose(
-                        banks[-1][:, g % 2, u, :], words[:, 256 * g + u : 256 * (g + 1) : 2], ident[:]
-                    )
+        def new_turned():
+            return psum.tile([P, 2, 2, TOKENS], F32, name="turned", tag="turned")
 
-        def scale_product(m, g, banks, grouped):
+        def turn(words, j, split):
+            bank = new_turned()
+            for i in range(2):
+                w0 = 256 * (2 * j + i)
+                for u in range(2):
+                    cols = slice(w0 + 128 * u, w0 + 128 * (u + 1)) if split else slice(w0 + u, w0 + 256, 2)
+                    nc.tensor.transpose(bank[:, i, u, :], words[:, cols], ident[:])
+            return bank
+
+        def turn_x(m, j):
+            return turn(xwide[m][:].bitcast(F32), j, False)
+
+        def scale_product(m, g, bank, grouped):
             nc.vector.tensor_tensor(
                 out=grouped[:, g * K_PASS : (g + 1) * K_PASS].rearrange("p (r u e) -> p r u e", u=2, e=2),
-                in0=banks[g // 2][:, g % 2, :, :].bitcast(BF16).rearrange("p u (r e) -> p r u e", e=2),
+                in0=bank[:, g % 2, :, :].bitcast(BF16).rearrange("p u (r e) -> p r u e", e=2),
                 in1=scale_x[:, g, :].rearrange("p (u e) -> p u e", u=2).unsqueeze(1).to_broadcast([P, TOKENS, 2, 2]),
                 op=ALU.mult,
             )
@@ -112,78 +125,78 @@ def tile_multiheadattention_pb_w4_kernel(
         def new_acc():
             return psum.tile([TOKENS, N_TILE], F32, name="acc", tag="acc")
 
-        def mx_pass(acc, codes, plane, w, s, g, c):
+        def warm_tensor(count):
+            acc = new_acc()
+            for i in range(count):
+                nc.tensor.matmul(acc[:], lhsT=zeros[:, :P], rhs=zeros[:], start=True, stop=True)
+
+        def mx_pass(acc, codes, plane, w, s, g, n0, width):
             nc.tensor.matmul_mx(
-                out=acc[:],
+                out=acc,
                 lhsT=codes[:, g, :].bitcast(FP8X4),
                 lhsT_scale=plane[:, g, :],
-                rhs=w[:, g, 2 * c * N_TILE : 2 * (c + 1) * N_TILE].bitcast(FP4X4),
-                rhs_scale=s[:, g, c * N_TILE : (c + 1) * N_TILE],
+                rhs=w[:, g, 2 * n0 : 2 * (n0 + width)].bitcast(FP4X4),
+                rhs_scale=s[:, g, n0 : n0 + width],
                 start=(g == 0),
                 stop=(g == PASSES - 1),
             )
 
-        def gate_matmuls(m, together):
-            accs = []
-            for c0 in range(0, CHUNKS, together):
-                new = [new_acc() for c in range(together)]
-                for g in range(PASSES):
-                    for j in range(together):
-                        mx_pass(new[j], xcodes[m], xplane[m], gate_w, gate_s, g, c0 + j)
-                accs.extend(new)
+        def gate_matmuls(m, chunks):
+            accs = [new_acc() for c in chunks]
+            for g in range(PASSES):
+                for acc, c in zip(accs, chunks):
+                    mx_pass(acc[:], xcodes[m], xplane[m], gate_w, gate_s, g, c * N_TILE, N_TILE)
             return accs
 
         def sigmoids(accs):
             gates = []
             for acc in accs:
-                gate = work.tile([TOKENS, N_TILE], F32, name="gate", tag="gate", bufs=6)
+                gate = work.tile([TOKENS, N_TILE], F32, name="gate", tag="gate", bufs=12)
                 nc.scalar.activation(gate[:], acc[:], ACT.Sigmoid)
                 gates.append(gate)
             return gates
 
-        def products(m, gates):
-            h = work.tile([TOKENS, K], BF16, name="h", tag="h", bufs=3, align_bytes=64)
-            for c in range(CHUNKS):
-                cols = slice(c * N_TILE, (c + 1) * N_TILE)
+        def new_h():
+            return work.tile([TOKENS, K], BF16, name="h", tag="h", bufs=3, align_bytes=64)
+
+        def products(m, h, half, gates):
+            for j in range(2):
+                cols = slice((2 * half + j) * N_TILE, (2 * half + j + 1) * N_TILE)
                 nc.vector.tensor_tensor(
                     out=h[:, cols].rearrange("r (u p e) -> r u p e", u=2, e=2),
-                    in0=gates[c][:].rearrange("r (p u e) -> r u p e", u=2, e=2),
+                    in0=gates[j][:].rearrange("r (p u e) -> r u p e", u=2, e=2),
                     in1=y[m][:, cols].rearrange("r (p u e) -> r u p e", u=2, e=2),
                     op=ALU.mult,
                 )
-            return h
 
         def turn_h(h):
-            words = h[:].bitcast(F32)
-            banks = []
-            for g in range(PASSES):
-                if g % 2 == 0:
-                    banks.append(psum.tile([P, 2, 2, TOKENS], F32, name="turned", tag="turned"))
-                for u in range(2):
-                    nc.tensor.transpose(
-                        banks[-1][:, g % 2, u, :], words[:, 256 * g + 128 * u : 256 * g + 128 * (u + 1)], ident[:]
-                    )
-            return banks
+            return [turn(h[:].bitcast(F32), j, True) for j in range(2)]
 
-        def regroup(banks, copies):
-            grouped = work.tile([P, TOKENS * K // P], BF16, name="hgrouped", tag="hgrouped", bufs=2, align_bytes=64)
-            words = grouped[:].bitcast(F32)
-            for j in range(2):
-                copies[j](
-                    out=words[:, 512 * j : 512 * (j + 1)].rearrange("p (g r u) -> p g r u", g=2, u=2),
-                    in_=banks[j][:].rearrange("p g u r -> p g r u"),
-                )
-            return grouped
+        def new_hgrouped():
+            return work.tile([P, TOKENS * K // P], BF16, name="hgrouped", tag="hgrouped", bufs=2, align_bytes=64)
 
-        def project(m):
-            for c in range(CHUNKS):
+        def regroup(grouped, banks, j, copy):
+            copy(
+                out=grouped[:].bitcast(F32)[:, 512 * j : 512 * (j + 1)].rearrange("p (g r u) -> p g r u", g=2, u=2),
+                in_=banks[j][:].rearrange("p g u r -> p g r u"),
+            )
+
+        def empty_bank(m, acc, n0, width, on_scalar):
+            result = work.tile([TOKENS, N_TILE], F32, name="result", tag="result", bufs=8)
+            copy = nc.scalar.copy if on_scalar else nc.vector.tensor_copy
+            copy(out=result[:, :width], in_=acc)
+            queue = nc.scalar if on_scalar and width < N_TILE else nc.sync
+            queue.dma_start(out=out[m][:, n0 : n0 + width], in_=result[:, :width])
+
+        def project(m, banks, scalar_banks=(1, 3)):
+            n0 = 0
+            for i, (groups, width) in enumerate(banks):
                 acc = new_acc()
-                for g in range(PASSES):
-                    mx_pass(acc, hcodes[m], hplane[m], proj_w, proj_s, g, c)
-                result = work.tile([TOKENS, N_TILE], F32, name="result", tag="result", bufs=6)
-                copy = nc.vector.tensor_copy if c % 2 == 0 else nc.scalar.copy
-                copy(out=result[:], in_=acc[:])
-                nc.sync.dma_start(out=out[m][:, c * N_TILE : (c + 1) * N_TILE], in_=result[:])
+                for j in range(groups):
+                    for g in range(PASSES):
+                        mx_pass(acc[:, j * width : (j + 1) * width], hcodes[m], hplane[m], proj_w, proj_s, g, n0 + j * width, width)
+                empty_bank(m, acc[:, : groups * width], n0, groups * width, i in scalar_banks)
+                n0 += groups * width
 
         def new_xgrouped():
             return work.tile([P, TOKENS * K // P], BF16, name="xgrouped", tag="xgrouped", bufs=2, align_bytes=64)
@@ -191,56 +204,98 @@ def tile_multiheadattention_pb_w4_kernel(
         def prepare_x(m, banks):
             grouped = new_xgrouped()
             for g in range(PASSES):
-                scale_product(m, g, banks, grouped)
+                scale_product(m, g, banks[g // 2], grouped)
                 if g > 0:
                     quantize(xcodes[m], xplane[m], grouped, g - 1, g)
             quantize(xcodes[m], xplane[m], grouped, PASSES - 1, PASSES)
+
+        whole = [(1, N_TILE)] * CHUNKS
+
+        low, high = (0, 1), (2, 3)
 
         for g in range(PASSES):
             widen(0, g, nc.vector.tensor_copy if g < 2 else nc.scalar.copy)
         for g in range(PASSES):
             widen(1, g, nc.scalar.copy)
-        banks0 = []
-        turn_x(0, banks0)
-        grouped0 = new_xgrouped()
-        for g in range(PASSES):
-            scale_product(0, g, banks0, grouped0)
-            quantize(xcodes[0], xplane[0], grouped0, g, g + 1)
-        banks1 = []
-        turn_x(1, banks1)
-        prepare_x(1, banks1)
-        accs0 = gate_matmuls(0, 4)
+        warm_tensor(5)
+        banks0 = [turn_x(0, j) for j in range(2)]
+        banks1 = [turn_x(1, j) for j in range(2)]
+        grouped0, grouped1 = new_xgrouped(), new_xgrouped()
 
-        for g in range(PASSES):
-            widen(2, g, nc.scalar.copy)
-        banks2 = []
-        turn_x(2, banks2)
-        h0 = products(0, sigmoids(accs0))
+        def product_0(g):
+            scale_product(0, g, banks0[g // 2], grouped0)
+
+        def quantize_0(g):
+            quantize(xcodes[0], xplane[0], grouped0, g, g + 1)
+
+        product_0(0)
+        quantize_0(0)
+        product_0(1)
+        product_0(2)
+        quantize_0(1)
+        product_0(3)
+        quantize_0(2)
+        scale_product(1, 0, banks1[0], grouped1)
+        quantize_0(3)
+        for g in range(1, PASSES):
+            scale_product(1, g, banks1[g // 2], grouped1)
+            quantize(xcodes[1], xplane[1], grouped1, g - 1, g)
+        quantize(xcodes[1], xplane[1], grouped1, PASSES - 1, PASSES)
+        accs0 = gate_matmuls(0, low + high)
+        widen(2, 0, nc.scalar.copy)
+        widen(2, 1, nc.scalar.copy)
+        gates_a0 = sigmoids(accs0[:2])
+        widen(2, 2, nc.scalar.copy)
+        widen(2, 3, nc.scalar.copy)
+        gates_b0 = sigmoids(accs0[2:])
+        a1 = gate_matmuls(1, low)
+        banks2 = [turn_x(2, j) for j in range(2)]
+        h0 = new_h()
+        products(0, h0, 0, gates_a0)
+        products(0, h0, 1, gates_b0)
         prepare_x(2, banks2)
-        accs1 = gate_matmuls(1, 2)
+        gates_a1 = sigmoids(a1)
         for g in range(PASSES):
             widen(3, g, nc.scalar.copy)
-        h1 = products(1, sigmoids(accs1))
+        b1 = gate_matmuls(1, high)
+        gates_b1 = sigmoids(b1)
+        a2 = gate_matmuls(2, low)
         hbanks0 = turn_h(h0)
-        banks3 = []
-        turn_x(3, banks3)
-        hgrouped0 = regroup(hbanks0, (nc.scalar.copy, nc.scalar.copy))
+        banks3 = [turn_x(3, j) for j in range(2)]
+        h1 = new_h()
+        products(1, h1, 0, gates_a1)
+        products(1, h1, 1, gates_b1)
+        gates_a2 = sigmoids(a2)
+        hgrouped0 = new_hgrouped()
+        for j in range(2):
+            regroup(hgrouped0, hbanks0, j, nc.scalar.copy)
         quantize(hcodes[0], hplane[0], hgrouped0, 0, PASSES)
         prepare_x(3, banks3)
-        accs2 = gate_matmuls(2, 2)
-        h2 = products(2, sigmoids(accs2))
-        project(0)
+        b2 = gate_matmuls(2, high)
+        gates_b2 = sigmoids(b2)
+        h2 = new_h()
+        products(2, h2, 0, gates_a2)
+        products(2, h2, 1, gates_b2)
+        project(0, whole, range(CHUNKS))
         hbanks1 = turn_h(h1)
         hbanks2 = turn_h(h2)
-        hgrouped1 = regroup(hbanks1, (nc.scalar.copy, nc.vector.tensor_copy))
-        hgrouped2 = regroup(hbanks2, (nc.scalar.copy, nc.vector.tensor_copy))
-        quantize(hcodes[1], hplane[1], hgrouped1, 0, PASSES)
-        quantize(hcodes[2], hplane[2], hgrouped2, 0, PASSES)
-        accs3 = gate_matmuls(3, 2)
-        h3 = products(3, sigmoids(accs3))
-        project(1)
+        for m, hbanks in ((1, hbanks1), (2, hbanks2)):
+            hgrouped = new_hgrouped()
+            regroup(hgrouped, hbanks, 0, nc.scalar.copy)
+            regroup(hgrouped, hbanks, 1, nc.vector.tensor_copy)
+            quantize(hcodes[m], hplane[m], hgrouped, 0, PASSES)
+        a3 = gate_matmuls(3, low)
+        gates_a3 = sigmoids(a3)
+        b3 = gate_matmuls(3, high)
+        gates_b3 = sigmoids(b3)
+        h3 = new_h()
+        products(3, h3, 0, gates_a3)
+        products(3, h3, 1, gates_b3)
+        project(1, whole)
         hbanks3 = turn_h(h3)
-        hgrouped3 = regroup(hbanks3, (nc.scalar.copy, nc.vector.tensor_copy))
+        hgrouped3 = new_hgrouped()
+        regroup(hgrouped3, hbanks3, 0, nc.scalar.copy)
+        regroup(hgrouped3, hbanks3, 1, nc.vector.tensor_copy)
         quantize(hcodes[3], hplane[3], hgrouped3, 0, PASSES)
-        project(2)
-        project(3)
+        project(2, whole)
+        project(3, whole[:-1] + [(2, N_TILE // 4)] * 2, (1, 4))

from contextlib import ExitStack

import concourse.mybir as mybir
from concourse.masks import make_identity

BATCH, TOKENS, K = 4, 128, 2048
P = 128
PACK = 4
K_PASS = P * PACK
PASSES = K // K_PASS
N_TILE = 512
CHUNKS = K // N_TILE

FLOPS = 2 * 2 * BATCH * TOKENS * K * K

F32 = mybir.dt.float32
BF16 = mybir.dt.bfloat16
I32 = mybir.dt.int32
U32 = mybir.dt.uint32
U8 = mybir.dt.uint8
FP8 = mybir.dt.float8_e4m3fn
FP8X4 = mybir.dt.float8_e4m3fn_x4
FP4X4 = mybir.dt.float4_e2m1fn_x4
ACT = mybir.ActivationFunctionType
ALU = mybir.AluOpType


def tile_multiheadattention_pb_w4_kernel(
    tc, x_bytes, x_scale, y_attn, w_gate_words, w_gate_scales, w_proj_words, w_proj_scales, out
):
    nc = tc.nc
    with ExitStack() as ctx:
        keep = ctx.enter_context(tc.tile_pool(name="keep", bufs=1))
        work = ctx.enter_context(tc.tile_pool(name="work", bufs=2))
        psum = ctx.enter_context(tc.psum_pool(name="psum", bufs=4))
        ctx.enter_context(tc.manual_schedule())

        ident = keep.tile([P, P], F32, name="ident")
        scale_x = keep.tile([P, PASSES, PACK], F32, name="scale_x")
        zeros = keep.tile([P, N_TILE], BF16, name="zeros", align_bytes=64)
        warm = keep.tile([P, 1], F32, name="warm")
        gate_w = keep.tile([P, PASSES, 2 * K], U8, name="gate_w", align_bytes=64)
        gate_s = keep.tile([P, PASSES, K], U8, name="gate_s", align_bytes=64)
        proj_w = keep.tile([P, PASSES, 2 * K], U8, name="proj_w", align_bytes=64)
        proj_s = keep.tile([P, PASSES, K], U8, name="proj_s", align_bytes=64)
        xraw = [keep.tile([P, K], U8, name="xraw%d" % m, align_bytes=64) for m in range(BATCH)]
        y = [keep.tile([P, K], BF16, name="y%d" % m, align_bytes=64) for m in range(BATCH)]
        xwide = [keep.tile([P, K], BF16, name="xwide%d" % m, align_bytes=64) for m in range(BATCH)]
        xcodes = [keep.tile([P, PASSES, TOKENS], U32, name="xcodes%d" % m, align_bytes=64) for m in range(BATCH)]
        xplane = [keep.tile([P, PASSES, TOKENS], U8, name="xplane%d" % m, align_bytes=64) for m in range(BATCH)]
        hcodes = [keep.tile([P, PASSES, TOKENS], U32, name="hcodes%d" % m, align_bytes=64) for m in range(BATCH)]
        hplane = [keep.tile([P, PASSES, TOKENS], U8, name="hplane%d" % m, align_bytes=64) for m in range(BATCH)]

        def load_scales(plane, scales):
            for r in range(4):
                nc.sync.dma_start(
                    out=plane[r:P:32, :, :].bitcast(I32),
                    in_=scales[:, r::4, :].rearrange("g q n -> q g n").bitcast(I32),
                )

        def load_words(tile, words, g0, g1):
            nc.sync.dma_start(out=tile[:, g0:g1, :], in_=words[g0:g1].rearrange("g p b -> p g b"))

        def load_y(m):
            nc.sync.dma_start(out=y[m][:], in_=y_attn[m].rearrange("t h d -> t (h d)"))

        nc.scalar.dma_start(out=scale_x[:], in_=x_scale.rearrange("a b (g p t) -> p (a b g) t", p=P, t=PACK))
        make_identity(nc, ident[:])
        nc.gpsimd.memset(zeros[:], 0.0)
        nc.vector.memset(gate_s[:].rearrange("p g n -> p (g n)").bitcast(I32), 0)
        nc.vector.memset(warm[:], 0.0)
        nc.scalar.activation(warm[:], warm[:], ACT.Sigmoid)
        for half in range(2):
            cols = slice(half * K // 2, (half + 1) * K // 2)
            nc.sync.dma_start(out=xraw[0][:, cols], in_=x_bytes[0][:, cols])
        nc.sync.dma_start(out=xraw[1][:], in_=x_bytes[1])
        load_scales(gate_s, w_gate_scales)
        for g in range(PASSES):
            load_words(gate_w, w_gate_words, g, g + 1)
        nc.sync.dma_start(out=xraw[2][:], in_=x_bytes[2])
        load_y(0)
        nc.sync.dma_start(out=xraw[3][:], in_=x_bytes[3])
        load_y(1)
        nc.vector.memset(proj_s[:].rearrange("p g n -> p (g n)").bitcast(I32), 0)
        load_scales(proj_s, w_proj_scales)
        for g in range(0, PASSES, 2):
            load_words(proj_w, w_proj_words, g, g + 2)
        for m in range(2, BATCH):
            load_y(m)

        def widen(m, g, copy):
            cols = slice(g * K_PASS, (g + 1) * K_PASS)
            copy(out=xwide[m][:, cols], in_=xraw[m][:, cols].bitcast(FP8))

        def new_turned():
            return psum.tile([P, 2, 2, TOKENS], F32, name="turned", tag="turned")

        def turn(words, j, split):
            bank = new_turned()
            for i in range(2):
                w0 = 256 * (2 * j + i)
                for u in range(2):
                    cols = slice(w0 + 128 * u, w0 + 128 * (u + 1)) if split else slice(w0 + u, w0 + 256, 2)
                    nc.tensor.transpose(bank[:, i, u, :], words[:, cols], ident[:])
            return bank

        def turn_x(m, j):
            return turn(xwide[m][:].bitcast(F32), j, False)

        def scale_product(m, g, bank, grouped):
            nc.vector.tensor_tensor(
                out=grouped[:, g * K_PASS : (g + 1) * K_PASS].rearrange("p (r u e) -> p r u e", u=2, e=2),
                in0=bank[:, g % 2, :, :].bitcast(BF16).rearrange("p u (r e) -> p r u e", e=2),
                in1=scale_x[:, g, :].rearrange("p (u e) -> p u e", u=2).unsqueeze(1).to_broadcast([P, TOKENS, 2, 2]),
                op=ALU.mult,
            )

        def quantize(codes, plane, grouped, g0, g1):
            nc.vector.quantize_mx(
                out=codes[:, g0:g1, :].rearrange("p g r -> p (g r)").bitcast(FP8X4),
                scales=plane[:, g0:g1, :].rearrange("p g r -> p (g r)"),
                in_=grouped[:, g0 * K_PASS : g1 * K_PASS],
            )

        def new_acc():
            return psum.tile([TOKENS, N_TILE], F32, name="acc", tag="acc")

        def warm_tensor(count):
            acc = new_acc()
            for i in range(count):
                nc.tensor.matmul(acc[:], lhsT=zeros[:, :P], rhs=zeros[:], start=True, stop=True)

        def mx_pass(acc, codes, plane, w, s, g, n0, width):
            nc.tensor.matmul_mx(
                out=acc,
                lhsT=codes[:, g, :].bitcast(FP8X4),
                lhsT_scale=plane[:, g, :],
                rhs=w[:, g, 2 * n0 : 2 * (n0 + width)].bitcast(FP4X4),
                rhs_scale=s[:, g, n0 : n0 + width],
                start=(g == 0),
                stop=(g == PASSES - 1),
            )

        def gate_matmuls(m, chunks):
            accs = [new_acc() for c in chunks]
            for g in range(PASSES):
                for acc, c in zip(accs, chunks):
                    mx_pass(acc[:], xcodes[m], xplane[m], gate_w, gate_s, g, c * N_TILE, N_TILE)
            return accs

        def sigmoids(accs):
            gates = []
            for acc in accs:
                gate = work.tile([TOKENS, N_TILE], F32, name="gate", tag="gate", bufs=12)
                nc.scalar.activation(gate[:], acc[:], ACT.Sigmoid)
                gates.append(gate)
            return gates

        def new_h():
            return work.tile([TOKENS, K], BF16, name="h", tag="h", bufs=3, align_bytes=64)

        def products(m, h, half, gates):
            for j in range(2):
                cols = slice((2 * half + j) * N_TILE, (2 * half + j + 1) * N_TILE)
                nc.vector.tensor_tensor(
                    out=h[:, cols].rearrange("r (u p e) -> r u p e", u=2, e=2),
                    in0=gates[j][:].rearrange("r (p u e) -> r u p e", u=2, e=2),
                    in1=y[m][:, cols].rearrange("r (p u e) -> r u p e", u=2, e=2),
                    op=ALU.mult,
                )

        def turn_h(h):
            return [turn(h[:].bitcast(F32), j, True) for j in range(2)]

        def new_hgrouped():
            return work.tile([P, TOKENS * K // P], BF16, name="hgrouped", tag="hgrouped", bufs=2, align_bytes=64)

        def regroup(grouped, banks, j, copy):
            copy(
                out=grouped[:].bitcast(F32)[:, 512 * j : 512 * (j + 1)].rearrange("p (g r u) -> p g r u", g=2, u=2),
                in_=banks[j][:].rearrange("p g u r -> p g r u"),
            )

        def empty_bank(m, acc, n0, width, on_scalar):
            result = work.tile([TOKENS, N_TILE], F32, name="result", tag="result", bufs=8)
            copy = nc.scalar.copy if on_scalar else nc.vector.tensor_copy
            copy(out=result[:, :width], in_=acc)
            queue = nc.scalar if on_scalar and width < N_TILE else nc.sync
            queue.dma_start(out=out[m][:, n0 : n0 + width], in_=result[:, :width])

        def project(m, banks, scalar_banks=(1, 3)):
            n0 = 0
            for i, (groups, width) in enumerate(banks):
                acc = new_acc()
                for j in range(groups):
                    for g in range(PASSES):
                        mx_pass(acc[:, j * width : (j + 1) * width], hcodes[m], hplane[m], proj_w, proj_s, g, n0 + j * width, width)
                empty_bank(m, acc[:, : groups * width], n0, groups * width, i in scalar_banks)
                n0 += groups * width

        def new_xgrouped():
            return work.tile([P, TOKENS * K // P], BF16, name="xgrouped", tag="xgrouped", bufs=2, align_bytes=64)

        def prepare_x(m, banks):
            grouped = new_xgrouped()
            for g in range(PASSES):
                scale_product(m, g, banks[g // 2], grouped)
                if g > 0:
                    quantize(xcodes[m], xplane[m], grouped, g - 1, g)
            quantize(xcodes[m], xplane[m], grouped, PASSES - 1, PASSES)

        whole = [(1, N_TILE)] * CHUNKS

        low, high = (0, 1), (2, 3)

        for g in range(PASSES):
            widen(0, g, nc.vector.tensor_copy if g < 2 else nc.scalar.copy)
        for g in range(PASSES):
            widen(1, g, nc.scalar.copy)
        warm_tensor(5)
        banks0 = [turn_x(0, j) for j in range(2)]
        banks1 = [turn_x(1, j) for j in range(2)]
        grouped0, grouped1 = new_xgrouped(), new_xgrouped()

        def product_0(g):
            scale_product(0, g, banks0[g // 2], grouped0)

        def quantize_0(g):
            quantize(xcodes[0], xplane[0], grouped0, g, g + 1)

        product_0(0)
        quantize_0(0)
        product_0(1)
        product_0(2)
        quantize_0(1)
        product_0(3)
        quantize_0(2)
        scale_product(1, 0, banks1[0], grouped1)
        quantize_0(3)
        for g in range(1, PASSES):
            scale_product(1, g, banks1[g // 2], grouped1)
            quantize(xcodes[1], xplane[1], grouped1, g - 1, g)
        quantize(xcodes[1], xplane[1], grouped1, PASSES - 1, PASSES)
        accs0 = gate_matmuls(0, low + high)
        widen(2, 0, nc.scalar.copy)
        widen(2, 1, nc.scalar.copy)
        gates_a0 = sigmoids(accs0[:2])
        widen(2, 2, nc.scalar.copy)
        widen(2, 3, nc.scalar.copy)
        gates_b0 = sigmoids(accs0[2:])
        a1 = gate_matmuls(1, low)
        banks2 = [turn_x(2, j) for j in range(2)]
        h0 = new_h()
        products(0, h0, 0, gates_a0)
        products(0, h0, 1, gates_b0)
        prepare_x(2, banks2)
        gates_a1 = sigmoids(a1)
        for g in range(PASSES):
            widen(3, g, nc.scalar.copy)
        b1 = gate_matmuls(1, high)
        gates_b1 = sigmoids(b1)
        a2 = gate_matmuls(2, low)
        hbanks0 = turn_h(h0)
        banks3 = [turn_x(3, j) for j in range(2)]
        h1 = new_h()
        products(1, h1, 0, gates_a1)
        products(1, h1, 1, gates_b1)
        gates_a2 = sigmoids(a2)
        hgrouped0 = new_hgrouped()
        for j in range(2):
            regroup(hgrouped0, hbanks0, j, nc.scalar.copy)
        quantize(hcodes[0], hplane[0], hgrouped0, 0, PASSES)
        prepare_x(3, banks3)
        b2 = gate_matmuls(2, high)
        gates_b2 = sigmoids(b2)
        h2 = new_h()
        products(2, h2, 0, gates_a2)
        products(2, h2, 1, gates_b2)
        project(0, whole, range(CHUNKS))
        hbanks1 = turn_h(h1)
        hbanks2 = turn_h(h2)
        for m, hbanks in ((1, hbanks1), (2, hbanks2)):
            hgrouped = new_hgrouped()
            regroup(hgrouped, hbanks, 0, nc.scalar.copy)
            regroup(hgrouped, hbanks, 1, nc.vector.tensor_copy)
            quantize(hcodes[m], hplane[m], hgrouped, 0, PASSES)
        a3 = gate_matmuls(3, low)
        gates_a3 = sigmoids(a3)
        b3 = gate_matmuls(3, high)
        gates_b3 = sigmoids(b3)
        h3 = new_h()
        products(3, h3, 0, gates_a3)
        products(3, h3, 1, gates_b3)
        project(1, whole)
        hbanks3 = turn_h(h3)
        hgrouped3 = new_hgrouped()
        regroup(hgrouped3, hbanks3, 0, nc.scalar.copy)
        regroup(hgrouped3, hbanks3, 1, nc.vector.tensor_copy)
        quantize(hcodes[3], hplane[3], hgrouped3, 0, PASSES)
        project(2, whole)
        project(3, whole[:-1] + [(2, N_TILE // 4)] * 2, (1, 4))
